import numpy as np
import ml_dtypes


def mxq(x, axis, fmt="e4m3"):
    dtype, down = {"e4m3": (ml_dtypes.float8_e4m3fn, 7), "e5m2": (ml_dtypes.float8_e5m2, 14)}[fmt]
    v = np.moveaxis(np.asarray(x, np.float32).astype(ml_dtypes.bfloat16).astype(np.float64), axis, -1)
    blocks = v.reshape(v.shape[:-1] + (-1, 32))
    amax = np.abs(blocks).max(-1, keepdims=True)
    byte = np.maximum(np.where(amax > 0, np.frexp(amax)[1] - 1 + 127, 0) - down, 1)
    scale = np.exp2(byte - 127.0)
    codes = (blocks / scale).astype(np.float32).astype(dtype).astype(np.float64)
    return np.moveaxis((codes * scale).reshape(v.shape), -1, axis)


WIDE = False


def mx_kscale(k):
    if not WIDE:
        return np.ones(k)
    levels = np.array([10, -10, 5, -5, 0])
    a = np.random.permutation(np.resize(levels, k // 512 * 4)).reshape(k // 512, 4)
    idx = np.arange(k)
    return np.exp2(a[idx // 512, idx % 128 // 32])


BF16 = ml_dtypes.bfloat16


def bf(x):
    return np.asarray(x, np.float32).astype(BF16)


def f64(x):
    return np.asarray(x).astype(np.float64)


N, MI, MO, LMAX = 128, 512, 128, 3
C = (LMAX + 1) ** 2


def setup_inputs():
    s = mx_kscale(MI)
    d = {"x": bf(np.random.standard_normal((N, MI, C)) * s[None, :, None])}
    for l in range(LMAX + 1):
        d["w%d" % l] = bf(np.random.standard_normal((MI, MO)) / np.sqrt(MI) / s[:, None])
    return d


def reference(x, w0, w1, w2, w3):
    xq = mxq(f64(x), 1, "e4m3")
    parts = []
    for l, w in enumerate([w0, w1, w2, w3]):
        xl = xq[:, :, l * l:(l + 1) ** 2].transpose(0, 2, 1)
        parts.append((xl @ mxq(f64(w), 0, "e4m3")).transpose(0, 2, 1))
    return np.concatenate(parts, axis=2)

@@ -1,0 +1,132 @@
+from contextlib import ExitStack
+
+import concourse.mybir as mybir
+from concourse.masks import make_identity
+
+BF16 = mybir.dt.bfloat16
+F32 = mybir.dt.float32
+U32 = mybir.dt.uint32
+U8 = mybir.dt.uint8
+FP8X4 = mybir.dt.float8_e4m3fn_x4
+
+P = 128
+PACK = 4
+N, MI, MO, LMAX = 128, 512, 128, 3
+C = (LMAX + 1) ** 2
+DEGREES = LMAX + 1
+HALVES = 2
+I_ROW = MI // HALVES
+N_HALF = P // HALVES
+X_PARTS = N // N_HALF
+LOADS_PER_PART = 4
+I_LOAD = I_ROW // LOADS_PER_PART
+GROUP = 4
+GROUPS = C // GROUP
+
+FLOPS = 2 * N * MI * MO * C
+
+
+def tile_irrepsstridelinear_s_kernel(tc, x, w0, w1, w2, w3, out):
+    nc = tc.nc
+    weights = [w0, w1, w2, w3]
+    degree_of_channel = [l for l in range(DEGREES) for m in range(2 * l + 1)]
+
+    with ExitStack() as ctx:
+        keep = ctx.enter_context(tc.tile_pool(name="keep", bufs=1))
+        psum_t = ctx.enter_context(tc.psum_pool(name="psum_t", bufs=4))
+        psum_o = ctx.enter_context(tc.psum_pool(name="psum_o", bufs=4))
+
+        identity = keep.tile([P, P], F32)
+        make_identity(nc, identity[:])
+
+        w_raw = keep.tile([P, DEGREES, PACK, MO], BF16)
+        for l in range(DEGREES):
+            nc.sync.dma_start(
+                out=w_raw[:, l, :, :].rearrange("p (h e) o -> p h (e o)", h=HALVES),
+                in_=weights[l].rearrange("(h p e) o -> p h (e o)", h=HALVES, p=P),
+            )
+        x_rows = x.rearrange("n (h i) c -> (n h) (i c)", h=HALVES)
+        x_raw = []
+        for g in range(X_PARTS):
+            x_raw.append(keep.tile([P, I_ROW, C], BF16, name="x_raw%d" % g))
+            for q in range(LOADS_PER_PART):
+                nc.sync.dma_start(
+                    out=x_raw[g][:, q * I_LOAD : (q + 1) * I_LOAD, :].rearrange("p i c -> p (i c)"),
+                    in_=x_rows[g * P : (g + 1) * P, q * I_LOAD * C : (q + 1) * I_LOAD * C],
+                )
+
+        w_grouped = keep.tile([P, DEGREES, MO, PACK], BF16, align_bytes=64)
+        for l in range(DEGREES):
+            nc.scalar.copy(
+                out=w_grouped[:, l, :, :].rearrange("p (a b) t -> p a t b", b=4),
+                in_=w_raw[:, l, :, :].rearrange("p t (a b) -> p a t b", b=4),
+            )
+        w_codes = keep.tile([P, DEGREES * MO], U32, align_bytes=64)
+        w_scales = keep.tile([P, DEGREES * MO], U8, align_bytes=64)
+
+        x_by_channel = [
+            keep.tile([P, C, I_ROW], BF16, name="x_by_channel%d" % g) for g in range(X_PARTS)
+        ]
+        x_grouped = keep.tile([P, C, N * PACK], BF16, align_bytes=64)
+        x_grouped_words = x_grouped[:].bitcast(F32)
+
+        def sort_by_channel(g):
+            for q in range(LOADS_PER_PART):
+                i_range = slice(q * I_LOAD, (q + 1) * I_LOAD)
+                nc.vector.tensor_copy(
+                    out=x_by_channel[g][:, :, i_range].rearrange("p (a b) i -> p a i b", b=4),
+                    in_=x_raw[g][:, i_range, :].rearrange("p i (a b) -> p a i b", b=4),
+                )
+
+        def flip(g):
+            words = x_by_channel[g][:].bitcast(F32)
+            for a in range(GROUPS):
+                flipped = psum_t.tile([P, GROUP, P], F32)
+                for b in range(GROUP):
+                    nc.tensor.transpose(flipped[:, b, :], words[:, a * GROUP + b, :], identity[:])
+                nc.scalar.copy(
+                    out=x_grouped_words[:, a * GROUP : (a + 1) * GROUP, g * P : (g + 1) * P],
+                    in_=flipped[:],
+                )
+
+        sort_by_channel(0)
+        nc.vector.quantize_mx(
+            out=w_codes[:].bitcast(FP8X4),
+            scales=w_scales[:],
+            in_=w_grouped[:].rearrange("p l o t -> p (l o t)"),
+        )
+        flip(0)
+        sort_by_channel(1)
+        flip(1)
+
+        x_codes = keep.tile([P, C * N], U32, align_bytes=64)
+        x_scales = keep.tile([P, C * N], U8, align_bytes=64)
+        result = keep.tile([P, MO, C], F32)
+        for a in range(GROUPS):
+            columns = slice(a * GROUP * N, (a + 1) * GROUP * N)
+            nc.vector.quantize_mx(
+                out=x_codes[:, columns].bitcast(FP8X4),
+                scales=x_scales[:, columns],
+                in_=x_grouped[:, a * GROUP : (a + 1) * GROUP, :].rearrange("p c m -> p (c m)"),
+            )
+            acc = psum_o.tile([P, GROUP, MO], F32)
+            for b in range(GROUP):
+                c = a * GROUP + b
+                l = degree_of_channel[c]
+                nc.tensor.matmul_mx(
+                    out=acc[:, b, :],
+                    lhsT=x_codes[:, c * N : (c + 1) * N].bitcast(FP8X4),
+                    lhsT_scale=x_scales[:, c * N : (c + 1) * N],
+                    rhs=w_codes[:, l * MO : (l + 1) * MO].bitcast(FP8X4),
+                    rhs_scale=w_scales[:, l * MO : (l + 1) * MO],
+                    start=True,
+                    stop=True,
+                )
+            nc.scalar.copy(
+                out=result[:, :, a * GROUP : (a + 1) * GROUP],
+                in_=acc[:].rearrange("p b o -> p o b"),
+            )
+        nc.sync.dma_start(
+            out=out.rearrange("n o c -> n (o c)"),
+            in_=result[:].rearrange("p o c -> p (o c)"),
+        )

@@ -35,50 +35,38 @@ def tile_irrepsstridelinear_s_kernel(tc, x, w0, w1, w2, w3, out):
         keep = ctx.enter_context(tc.tile_pool(name="keep", bufs=1))
         psum_t = ctx.enter_context(tc.psum_pool(name="psum_t", bufs=4))
         psum_o = ctx.enter_context(tc.psum_pool(name="psum_o", bufs=4))
+        ctx.enter_context(tc.manual_schedule())
 
         identity = keep.tile([P, P], F32)
         make_identity(nc, identity[:])
 
+        x_rows = x.rearrange("n (h i) c -> (n h) (i c)", h=HALVES)
+        x_raw = [keep.tile([P, I_ROW, C], BF16, name="x_raw%d" % g) for g in range(X_PARTS)]
+        for g in range(X_PARTS):
+            for q in range(LOADS_PER_PART):
+                nc.sync.dma_start(
+                    out=x_raw[g][:, q * I_LOAD : (q + 1) * I_LOAD, :].rearrange("p i c -> p (i c)"),
+                    in_=x_rows[g * P : (g + 1) * P, q * I_LOAD * C : (q + 1) * I_LOAD * C],
+                )
         w_raw = keep.tile([P, DEGREES, PACK, MO], BF16)
         for l in range(DEGREES):
             nc.sync.dma_start(
                 out=w_raw[:, l, :, :].rearrange("p (h e) o -> p h (e o)", h=HALVES),
                 in_=weights[l].rearrange("(h p e) o -> p h (e o)", h=HALVES, p=P),
             )
-        x_rows = x.rearrange("n (h i) c -> (n h) (i c)", h=HALVES)
-        x_raw = []
-        for g in range(X_PARTS):
-            x_raw.append(keep.tile([P, I_ROW, C], BF16, name="x_raw%d" % g))
-            for q in range(LOADS_PER_PART):
-                nc.sync.dma_start(
-                    out=x_raw[g][:, q * I_LOAD : (q + 1) * I_LOAD, :].rearrange("p i c -> p (i c)"),
-                    in_=x_rows[g * P : (g + 1) * P, q * I_LOAD * C : (q + 1) * I_LOAD * C],
-                )
-
-        w_grouped = keep.tile([P, DEGREES, MO, PACK], BF16, align_bytes=64)
-        for l in range(DEGREES):
-            nc.scalar.copy(
-                out=w_grouped[:, l, :, :].rearrange("p (a b) t -> p a t b", b=4),
-                in_=w_raw[:, l, :, :].rearrange("p t (a b) -> p a t b", b=4),
-            )
-        w_codes = keep.tile([P, DEGREES * MO], U32, align_bytes=64)
-        w_scales = keep.tile([P, DEGREES * MO], U8, align_bytes=64)
 
         x_by_channel = [
             keep.tile([P, C, I_ROW], BF16, name="x_by_channel%d" % g) for g in range(X_PARTS)
         ]
         x_grouped = keep.tile([P, C, N * PACK], BF16, align_bytes=64)
         x_grouped_words = x_grouped[:].bitcast(F32)
-
-        def sort_by_channel(g):
+        for g in range(X_PARTS):
             for q in range(LOADS_PER_PART):
                 i_range = slice(q * I_LOAD, (q + 1) * I_LOAD)
                 nc.vector.tensor_copy(
                     out=x_by_channel[g][:, :, i_range].rearrange("p (a b) i -> p a i b", b=4),
                     in_=x_raw[g][:, i_range, :].rearrange("p i (a b) -> p a i b", b=4),
                 )
-
-        def flip(g):
             words = x_by_channel[g][:].bitcast(F32)
             for a in range(GROUPS):
                 flipped = psum_t.tile([P, GROUP, P], F32)
@@ -89,15 +77,19 @@ def tile_irrepsstridelinear_s_kernel(tc, x, w0, w1, w2, w3, out):
                     in_=flipped[:],
                 )
 
-        sort_by_channel(0)
+        w_grouped = keep.tile([P, DEGREES, MO, PACK], BF16, align_bytes=64)
+        for l in range(DEGREES):
+            nc.vector.tensor_copy(
+                out=w_grouped[:, l, :, :].rearrange("p (a b) t -> p a t b", b=4),
+                in_=w_raw[:, l, :, :].rearrange("p t (a b) -> p a t b", b=4),
+            )
+        w_codes = keep.tile([P, DEGREES * MO], U32, align_bytes=64)
+        w_scales = keep.tile([P, DEGREES * MO], U8, align_bytes=64)
         nc.vector.quantize_mx(
             out=w_codes[:].bitcast(FP8X4),
             scales=w_scales[:],
             in_=w_grouped[:].rearrange("p l o t -> p (l o t)"),
         )
-        flip(0)
-        sort_by_channel(1)
-        flip(1)
 
         x_codes = keep.tile([P, C * N], U32, align_bytes=64)
         x_scales = keep.tile([P, C * N], U8, align_bytes=64)

@@ -35,7 +35,6 @@ def tile_irrepsstridelinear_s_kernel(tc, x, w0, w1, w2, w3, out):
         keep = ctx.enter_context(tc.tile_pool(name="keep", bufs=1))
         psum_t = ctx.enter_context(tc.psum_pool(name="psum_t", bufs=4))
         psum_o = ctx.enter_context(tc.psum_pool(name="psum_o", bufs=4))
-        ctx.enter_context(tc.manual_schedule())
 
         identity = keep.tile([P, P], F32)
         make_identity(nc, identity[:])

@@ -63,8 +63,8 @@ def tile_irrepsstridelinear_s_kernel(tc, x, w0, w1, w2, w3, out):
             for q in range(LOADS_PER_PART):
                 i_range = slice(q * I_LOAD, (q + 1) * I_LOAD)
                 nc.vector.tensor_copy(
-                    out=x_by_channel[g][:, :, i_range].rearrange("p (a b) i -> p a i b", b=4),
-                    in_=x_raw[g][:, i_range, :].rearrange("p i (a b) -> p a i b", b=4),
+                    out=x_by_channel[g][:, :, i_range],
+                    in_=x_raw[g][:, i_range, :].rearrange("p i c -> p c i"),
                 )
             words = x_by_channel[g][:].bitcast(F32)
             for a in range(GROUPS):

from contextlib import ExitStack

import concourse.mybir as mybir
from concourse.masks import make_identity

BF16 = mybir.dt.bfloat16
F32 = mybir.dt.float32
U32 = mybir.dt.uint32
U8 = mybir.dt.uint8
FP8X4 = mybir.dt.float8_e4m3fn_x4

P = 128
PACK = 4
N, MI, MO, LMAX = 128, 512, 128, 3
C = (LMAX + 1) ** 2
DEGREES = LMAX + 1
HALVES = 2
I_ROW = MI // HALVES
N_HALF = P // HALVES
X_PARTS = N // N_HALF
LOADS_PER_PART = 4
I_LOAD = I_ROW // LOADS_PER_PART
GROUP = 4
GROUPS = C // GROUP

FLOPS = 2 * N * MI * MO * C


def tile_irrepsstridelinear_s_kernel(tc, x, w0, w1, w2, w3, out):
    nc = tc.nc
    weights = [w0, w1, w2, w3]
    degree_of_channel = [l for l in range(DEGREES) for m in range(2 * l + 1)]

    with ExitStack() as ctx:
        keep = ctx.enter_context(tc.tile_pool(name="keep", bufs=1))
        psum_t = ctx.enter_context(tc.psum_pool(name="psum_t", bufs=4))
        psum_o = ctx.enter_context(tc.psum_pool(name="psum_o", bufs=4))

        identity = keep.tile([P, P], F32)
        make_identity(nc, identity[:])

        x_rows = x.rearrange("n (h i) c -> (n h) (i c)", h=HALVES)
        x_raw = [keep.tile([P, I_ROW, C], BF16, name="x_raw%d" % g) for g in range(X_PARTS)]
        for g in range(X_PARTS):
            for q in range(LOADS_PER_PART):
                nc.sync.dma_start(
                    out=x_raw[g][:, q * I_LOAD : (q + 1) * I_LOAD, :].rearrange("p i c -> p (i c)"),
                    in_=x_rows[g * P : (g + 1) * P, q * I_LOAD * C : (q + 1) * I_LOAD * C],
                )
        w_raw = keep.tile([P, DEGREES, PACK, MO], BF16)
        for l in range(DEGREES):
            nc.sync.dma_start(
                out=w_raw[:, l, :, :].rearrange("p (h e) o -> p h (e o)", h=HALVES),
                in_=weights[l].rearrange("(h p e) o -> p h (e o)", h=HALVES, p=P),
            )

        x_by_channel = [
            keep.tile([P, C, I_ROW], BF16, name="x_by_channel%d" % g) for g in range(X_PARTS)
        ]
        x_grouped = keep.tile([P, C, N * PACK], BF16, align_bytes=64)
        x_grouped_words = x_grouped[:].bitcast(F32)
        for g in range(X_PARTS):
            for q in range(LOADS_PER_PART):
                i_range = slice(q * I_LOAD, (q + 1) * I_LOAD)
                nc.vector.tensor_copy(
                    out=x_by_channel[g][:, :, i_range],
                    in_=x_raw[g][:, i_range, :].rearrange("p i c -> p c i"),
                )
            words = x_by_channel[g][:].bitcast(F32)
            for a in range(GROUPS):
                flipped = psum_t.tile([P, GROUP, P], F32)
                for b in range(GROUP):
                    nc.tensor.transpose(flipped[:, b, :], words[:, a * GROUP + b, :], identity[:])
                nc.scalar.copy(
                    out=x_grouped_words[:, a * GROUP : (a + 1) * GROUP, g * P : (g + 1) * P],
                    in_=flipped[:],
                )

        w_grouped = keep.tile([P, DEGREES, MO, PACK], BF16, align_bytes=64)
        for l in range(DEGREES):
            nc.vector.tensor_copy(
                out=w_grouped[:, l, :, :].rearrange("p (a b) t -> p a t b", b=4),
                in_=w_raw[:, l, :, :].rearrange("p t (a b) -> p a t b", b=4),
            )
        w_codes = keep.tile([P, DEGREES * MO], U32, align_bytes=64)
        w_scales = keep.tile([P, DEGREES * MO], U8, align_bytes=64)
        nc.vector.quantize_mx(
            out=w_codes[:].bitcast(FP8X4),
            scales=w_scales[:],
            in_=w_grouped[:].rearrange("p l o t -> p (l o t)"),
        )

        x_codes = keep.tile([P, C * N], U32, align_bytes=64)
        x_scales = keep.tile([P, C * N], U8, align_bytes=64)
        result = keep.tile([P, MO, C], F32)
        for a in range(GROUPS):
            columns = slice(a * GROUP * N, (a + 1) * GROUP * N)
            nc.vector.quantize_mx(
                out=x_codes[:, columns].bitcast(FP8X4),
                scales=x_scales[:, columns],
                in_=x_grouped[:, a * GROUP : (a + 1) * GROUP, :].rearrange("p c m -> p (c m)"),
            )
            acc = psum_o.tile([P, GROUP, MO], F32)
            for b in range(GROUP):
                c = a * GROUP + b
                l = degree_of_channel[c]
                nc.tensor.matmul_mx(
                    out=acc[:, b, :],
                    lhsT=x_codes[:, c * N : (c + 1) * N].bitcast(FP8X4),
                    lhsT_scale=x_scales[:, c * N : (c + 1) * N],
                    rhs=w_codes[:, l * MO : (l + 1) * MO].bitcast(FP8X4),
                    rhs_scale=w_scales[:, l * MO : (l + 1) * MO],
                    start=True,
                    stop=True,
                )
            nc.scalar.copy(
                out=result[:, :, a * GROUP : (a + 1) * GROUP],
                in_=acc[:].rearrange("p b o -> p o b"),
            )
        nc.sync.dma_start(
            out=out.rearrange("n o c -> n (o c)"),
            in_=result[:].rearrange("p o c -> p (o c)"),
        )
